import numpy as np
import ml_dtypes


def mxq(x, axis, fmt="e4m3"):
    dtype, down = {"e4m3": (ml_dtypes.float8_e4m3fn, 7), "e5m2": (ml_dtypes.float8_e5m2, 14)}[fmt]
    v = np.moveaxis(np.asarray(x, np.float32).astype(ml_dtypes.bfloat16).astype(np.float64), axis, -1)
    blocks = v.reshape(v.shape[:-1] + (-1, 32))
    amax = np.abs(blocks).max(-1, keepdims=True)
    byte = np.maximum(np.where(amax > 0, np.frexp(amax)[1] - 1 + 127, 0) - down, 1)
    scale = np.exp2(byte - 127.0)
    codes = (blocks / scale).astype(np.float32).astype(dtype).astype(np.float64)
    return np.moveaxis((codes * scale).reshape(v.shape), -1, axis)


WIDE = False


def mx_kscale(k):
    if not WIDE:
        return np.ones(k)
    levels = np.array([10, -10, 5, -5, 0])
    if k % 512:
        return np.exp2(np.random.permutation(np.resize(levels, k // 32))).repeat(32)
    a = np.empty((k // 512, 16))
    for p in range(k // 512):
        a[p, :8] = np.random.permutation(np.resize(levels, 8))
        for g in range(8):
            far = levels[np.abs(levels - a[p, g]) >= 10]
            a[p, g + 8] = far[np.random.randint(len(far))]
    return np.exp2(a.ravel()).repeat(32)


BF16 = ml_dtypes.bfloat16


def bf(x):
    return np.asarray(x, np.float32).astype(BF16)


def f64(x):
    return np.asarray(x).astype(np.float64)


B, N, DIN, DH, DOUT, DIM = 4, 1024, 512, 512, 128, 512


def draw_ahat():
    g = np.random.standard_normal((N, N))
    u = np.random.standard_normal(N) * 0.5
    a = g - g.T + u[:, None] - u[None, :]
    m = (a > 0) + np.eye(N)
    dinv = 1.0 / np.sqrt(m.sum(0))
    return m * (dinv[:, None] * dinv[None, :])


def setup_inputs():
    s, t = mx_kscale(DIN), mx_kscale(N)
    r = np.random.standard_normal
    return {"x": bf((r((B, N, DIN)) * s / t[:, None]).reshape(B * N, DIN)),
            "ahat": bf(draw_ahat() * t[:, None]),
            "gcn1_w": bf(r((DIN, DH)) * 0.2 * np.sqrt(N / DIN) / s[:, None]),
            "gcn1_b": bf(r(DH) * 0.2)}


def reference(x, ahat, gcn1_w, gcn1_b):
    xb = f64(x).reshape(B, N, DIN)
    y = mxq(xb, 2, "e4m3") @ mxq(f64(gcn1_w), 0, "e4m3")
    h = (mxq(f64(ahat), 0, "e4m3").T @ mxq(y, 1, "e4m3")) + f64(gcn1_b)
    return np.maximum(h, 0.0)

@@ -1,0 +1,227 @@
+from contextlib import ExitStack
+
+import concourse.mybir as mybir
+from concourse.masks import make_identity
+
+F32 = mybir.dt.float32
+BF16 = mybir.dt.bfloat16
+U32 = mybir.dt.uint32
+U8 = mybir.dt.uint8
+FP8X4 = mybir.dt.float8_e4m3fn_x4
+
+P = 128
+PACK = 4
+K_PASS = P * PACK
+
+GRAPHS = 4
+NODES = 1024
+D_IN = 512
+D_HID = 512
+
+GROUP = K_PASS
+N_GROUPS = GRAPHS * NODES // GROUP
+PASSES = NODES // K_PASS
+F_CHUNK = 128
+F_CHUNKS = D_HID // F_CHUNK
+J_TILES = NODES // P
+N_BANKS = GRAPHS * J_TILES
+BANKS_PER_ROUND = N_BANKS // N_GROUPS
+AHEAD = 2
+LAG = 3
+
+FLOPS = 2 * GRAPHS * NODES * D_IN * D_HID + 2 * GRAPHS * NODES * NODES * D_HID
+
+
+def tile_gcn_pb_t_kernel(tc, x, ahat, gcn1_w, gcn1_b, out):
+    nc = tc.nc
+    out_rows = out.flatten_outer_dims()
+
+    with ExitStack() as stack:
+        consts = stack.enter_context(tc.tile_pool(name="consts", bufs=1))
+        adjacency = stack.enter_context(tc.tile_pool(name="adjacency", bufs=PASSES))
+        resident = stack.enter_context(tc.tile_pool(name="resident", bufs=N_GROUPS))
+        rotating = stack.enter_context(tc.tile_pool(name="rotating", bufs=3))
+        results = stack.enter_context(tc.tile_pool(name="results", bufs=3 * BANKS_PER_ROUND))
+        psum_xt = stack.enter_context(tc.psum_pool(name="psum_xt", bufs=2))
+        psum_y = stack.enter_context(tc.psum_pool(name="psum_y", bufs=3))
+        psum_out = stack.enter_context(tc.psum_pool(name="psum_out", bufs=3))
+        stack.enter_context(tc.manual_schedule())
+
+        x_raw = {}
+        x_grouped = {}
+        x_codes = {}
+        y_grouped = {}
+        y_codes = {}
+        a_raw = {}
+        a_grouped = {}
+        a_codes = {}
+        result = {}
+
+        def load_x(g):
+            raw = resident.tile([P, PACK * D_IN], BF16, tag="x_raw")
+            nc.sync.dma_start(
+                out=raw[:], in_=x[g * GROUP : (g + 1) * GROUP, :].rearrange("(p t) k -> p (t k)", t=PACK)
+            )
+            x_raw[g] = raw
+
+        def load_adjacency(g):
+            raw = adjacency.tile([P, PACK, NODES], BF16, tag="a_raw")
+            nc.sync.dma_start(
+                out=raw[:], in_=ahat[g * K_PASS : (g + 1) * K_PASS, :].rearrange("(p t) j -> p t j", t=PACK)
+            )
+            a_raw[g] = raw
+
+        bias_row = consts.tile([P, D_HID], BF16, tag="bias_row")
+        nc.vector.memset(bias_row[:], 0.0)
+
+        load_x(0)
+        w_raw = consts.tile([P, PACK, D_HID], BF16, tag="w_raw")
+        nc.sync.dma_start(out=w_raw[:], in_=gcn1_w.rearrange("(q t) c -> q t c", t=PACK))
+        load_x(1)
+        nc.sync.dma_start(out=bias_row[0:1, :], in_=gcn1_b.unsqueeze(0))
+        for g in range(PASSES):
+            load_adjacency(g)
+            load_x(AHEAD + g)
+        for g in range(AHEAD + PASSES, N_GROUPS):
+            load_x(g)
+
+        identity = consts.tile([P, P], F32, tag="identity")
+        make_identity(nc, identity[:])
+        ones = consts.tile([P, P], BF16, tag="ones")
+        nc.vector.memset(ones[:], 1.0)
+        warm = consts.tile([P, 1], F32, tag="warm")
+        nc.vector.memset(warm[:], 0.0)
+        nc.scalar.activation(out=warm[:], in_=warm[:], func=mybir.ActivationFunctionType.Relu)
+
+        def regroup(dst, src):
+            nc.vector.tensor_copy(
+                out=dst.rearrange("p (c i) t -> p c t i", i=4), in_=src.rearrange("p t (c i) -> p c t i", i=4)
+            )
+
+        def quantise(grouped, width, pool, tag):
+            codes = pool.tile([P, width], U32, tag=tag + "_codes", align_bytes=64)
+            scales = pool.tile([P, width], U8, tag=tag + "_scales", align_bytes=64)
+            nc.vector.quantize_mx(out=codes[:].bitcast(FP8X4), scales=scales[:], in_=grouped)
+            return codes, scales
+
+        def transpose_x(g):
+            words = x_raw[g][:].bitcast(F32)
+            grouped = rotating.tile([P, PACK * GROUP], BF16, tag="x_grouped", align_bytes=64)
+            grouped_words = grouped[:].bitcast(F32)
+            for pair in range(2):
+                xt = psum_xt.tile([P, 2, 2, P], F32, tag="xt")
+                for h in range(2):
+                    for u in range(2):
+                        t = 2 * pair + h
+                        nc.tensor.transpose(
+                            xt[:, h, u, :], words[:, t * 256 + u : (t + 1) * 256 : 2], identity[:]
+                        )
+                nc.scalar.copy(
+                    out=grouped_words[:, pair * 512 : (pair + 1) * 512].rearrange(
+                        "q (h n u) -> q h n u", h=2, n=P, u=2
+                    ),
+                    in_=xt[:].rearrange("q h u n -> q h n u"),
+                )
+            x_grouped[g] = grouped
+
+        def first_matmul(g, c):
+            if c == 0:
+                grouped = rotating.tile([P, D_HID, PACK], BF16, tag="y_grouped", align_bytes=64)
+                y_grouped[g] = grouped
+            codes, scales = x_codes[g]
+            f_cols = slice(c * F_CHUNK, (c + 1) * F_CHUNK)
+            y_bank = psum_y.tile([P, PACK, F_CHUNK], F32, tag="y_bank")
+            for t in range(PACK):
+                n_cols = slice(t * P, (t + 1) * P)
+                nc.tensor.matmul_mx(
+                    out=y_bank[:, t, :],
+                    lhsT=codes[:, n_cols].bitcast(FP8X4),
+                    lhsT_scale=scales[:, n_cols],
+                    rhs=w_codes[:, f_cols].bitcast(FP8X4),
+                    rhs_scale=w_scales[:, f_cols],
+                    start=True,
+                    stop=True,
+                )
+            nc.scalar.copy(out=y_grouped[g][:, f_cols, :], in_=y_bank[:].rearrange("n t f -> n f t"))
+
+        def second_matmul(n):
+            b = n // J_TILES
+            j_cols = slice((n % J_TILES) * P, (n % J_TILES + 1) * P)
+            out_bank = psum_out.tile([P, D_HID], F32, tag="out_bank")
+            for g in range(PASSES):
+                nc.tensor.matmul_mx(
+                    out=out_bank[:],
+                    lhsT=a_codes[g][0][:, j_cols].bitcast(FP8X4),
+                    lhsT_scale=a_codes[g][1][:, j_cols],
+                    rhs=y_codes[PASSES * b + g][0][:].bitcast(FP8X4),
+                    rhs_scale=y_codes[PASSES * b + g][1][:],
+                    start=(g == 0),
+                    stop=(g == PASSES - 1),
+                )
+            biased = results.tile([P, D_HID], F32, tag="result")
+            nc.vector.tensor_tensor(out=biased[:], in0=out_bank[:], in1=bias_all[:], op=mybir.AluOpType.add)
+            result[n] = biased
+
+        def regroup_adjacency(g, j_half):
+            if j_half == 0:
+                grouped = adjacency.tile([P, NODES, PACK], BF16, tag="a_grouped", align_bytes=64)
+                codes = adjacency.tile([P, NODES], U32, tag="a_codes", align_bytes=64)
+                scales = adjacency.tile([P, NODES], U8, tag="a_scales", align_bytes=64)
+                a_grouped[g] = grouped
+                a_codes[g] = (codes, scales)
+            j_cols = slice(j_half * (NODES // 2), (j_half + 1) * (NODES // 2))
+            regroup(a_grouped[g][:, j_cols, :], a_raw[g][:, :, j_cols])
+
+        def quantise_adjacency(g, j_half):
+            j_cols = slice(j_half * (NODES // 2), (j_half + 1) * (NODES // 2))
+            nc.vector.quantize_mx(
+                out=a_codes[g][0][:, j_cols].bitcast(FP8X4),
+                scales=a_codes[g][1][:, j_cols],
+                in_=a_grouped[g][:, j_cols, :].rearrange("p j t -> p (j t)"),
+            )
+
+        def relu_and_store(n, on_vector):
+            if on_vector:
+                nc.vector.tensor_scalar_max(out=result[n][:], in0=result[n][:], scalar1=0.0)
+            else:
+                nc.scalar.activation(out=result[n][:], in_=result[n][:], func=mybir.ActivationFunctionType.Relu)
+            nc.sync.dma_start(out=out_rows[n * P : (n + 1) * P, :], in_=result[n][:])
+
+        transpose_x(0)
+        w_grouped = consts.tile([P, D_HID, PACK], BF16, tag="w_grouped", align_bytes=64)
+        regroup(w_grouped[:], w_raw[:])
+        x_codes[0] = quantise(x_grouped[0][:], GROUP, rotating, "x")
+        w_codes, w_scales = quantise(w_grouped[:].rearrange("p c t -> p (c t)"), D_HID, consts, "w")
+        transpose_x(1)
+        bias_bank = psum_out.tile([P, D_HID], F32, tag="out_bank")
+        nc.tensor.matmul(out=bias_bank[:], lhsT=ones[:], rhs=bias_row[:], start=True, stop=True)
+        bias_all = consts.tile([P, D_HID], F32, tag="bias_all")
+        nc.scalar.copy(out=bias_all[:], in_=bias_bank[:])
+
+        fresh_pieces = []
+        for r in range(N_GROUPS + LAG):
+            first_active = r < N_GROUPS
+            if 1 <= r <= N_GROUPS:
+                y_codes[r - 1] = quantise(y_grouped[r - 1][:].rearrange("p f t -> p (f t)"), D_HID, resident, "y")
+            if r + 1 < N_GROUPS:
+                x_codes[r + 1] = quantise(x_grouped[r + 1][:], GROUP, rotating, "x")
+            for piece in fresh_pieces:
+                quantise_adjacency(*piece)
+            banks = [BANKS_PER_ROUND * (r - LAG) + i for i in range(BANKS_PER_ROUND)] if r >= LAG else []
+            for half in range(2):
+                if first_active:
+                    first_matmul(r, 2 * half)
+                    first_matmul(r, 2 * half + 1)
+                for n in banks[2 * half : 2 * half + 2]:
+                    second_matmul(n)
+            for n in banks:
+                relu_and_store(n, on_vector=(r + 1 < N_GROUPS and n % 2 == 1))
+            if r + AHEAD < N_GROUPS:
+                transpose_x(r + AHEAD)
+            fresh_pieces = []
+            if r == 0:
+                fresh_pieces = [(0, 0), (0, 1)]
+            if r == 1 or r == 2:
+                fresh_pieces = [(1, r - 1)]
+            for piece in fresh_pieces:
+                regroup_adjacency(*piece)

@@ -27,7 +27,9 @@ J_TILES = NODES // P
 N_BANKS = GRAPHS * J_TILES
 BANKS_PER_ROUND = N_BANKS // N_GROUPS
 AHEAD = 2
-LAG = 3
+LAG = 4
+HALVES = 2
+J_HALF = NODES // HALVES
 
 FLOPS = 2 * GRAPHS * NODES * D_IN * D_HID + 2 * GRAPHS * NODES * NODES * D_HID
 
@@ -42,9 +44,7 @@ def tile_gcn_pb_t_kernel(tc, x, ahat, gcn1_w, gcn1_b, out):
         resident = stack.enter_context(tc.tile_pool(name="resident", bufs=N_GROUPS))
         rotating = stack.enter_context(tc.tile_pool(name="rotating", bufs=3))
         results = stack.enter_context(tc.tile_pool(name="results", bufs=3 * BANKS_PER_ROUND))
-        psum_xt = stack.enter_context(tc.psum_pool(name="psum_xt", bufs=2))
-        psum_y = stack.enter_context(tc.psum_pool(name="psum_y", bufs=3))
-        psum_out = stack.enter_context(tc.psum_pool(name="psum_out", bufs=3))
+        psum = stack.enter_context(tc.psum_pool(name="psum", bufs=8))
         stack.enter_context(tc.manual_schedule())
 
         x_raw = {}
@@ -57,32 +57,37 @@ def tile_gcn_pb_t_kernel(tc, x, ahat, gcn1_w, gcn1_b, out):
         a_codes = {}
         result = {}
 
-        def load_x(g):
+        def load_x(g, pieces=1):
             raw = resident.tile([P, PACK * D_IN], BF16, tag="x_raw")
-            nc.sync.dma_start(
-                out=raw[:], in_=x[g * GROUP : (g + 1) * GROUP, :].rearrange("(p t) k -> p (t k)", t=PACK)
-            )
+            group = x[g * GROUP : (g + 1) * GROUP, :].rearrange("(p t) k -> p (t k)", t=PACK)
+            width = PACK * D_IN // pieces
+            for i in range(pieces):
+                cols = slice(i * width, (i + 1) * width)
+                nc.sync.dma_start(out=raw[:, cols], in_=group[:, cols])
             x_raw[g] = raw
 
-        def load_adjacency(g):
-            raw = adjacency.tile([P, PACK, NODES], BF16, tag="a_raw")
-            nc.sync.dma_start(
-                out=raw[:], in_=ahat[g * K_PASS : (g + 1) * K_PASS, :].rearrange("(p t) j -> p t j", t=PACK)
-            )
-            a_raw[g] = raw
+        def load_adjacency(half):
+            j_cols = slice(half * J_HALF, (half + 1) * J_HALF)
+            for g in range(PASSES):
+                if half == 0:
+                    raw = adjacency.tile([P, PACK, NODES], BF16, tag="a_raw")
+                    a_raw[g] = raw
+                rows = ahat[g * K_PASS : (g + 1) * K_PASS, :].rearrange("(p t) j -> p t j", t=PACK)
+                nc.sync.dma_start(out=a_raw[g][:, :, j_cols], in_=rows[:, :, j_cols])
 
         bias_row = consts.tile([P, D_HID], BF16, tag="bias_row")
         nc.vector.memset(bias_row[:], 0.0)
 
-        load_x(0)
+        load_x(0, pieces=2)
         w_raw = consts.tile([P, PACK, D_HID], BF16, tag="w_raw")
         nc.sync.dma_start(out=w_raw[:], in_=gcn1_w.rearrange("(q t) c -> q t c", t=PACK))
-        load_x(1)
         nc.sync.dma_start(out=bias_row[0:1, :], in_=gcn1_b.unsqueeze(0))
-        for g in range(PASSES):
-            load_adjacency(g)
-            load_x(AHEAD + g)
-        for g in range(AHEAD + PASSES, N_GROUPS):
+        load_x(1)
+        load_x(2)
+        load_adjacency(0)
+        load_x(3)
+        load_adjacency(1)
+        for g in range(4, N_GROUPS):
             load_x(g)
 
         identity = consts.tile([P, P], F32, tag="identity")
@@ -109,7 +114,7 @@ def tile_gcn_pb_t_kernel(tc, x, ahat, gcn1_w, gcn1_b, out):
             grouped = rotating.tile([P, PACK * GROUP], BF16, tag="x_grouped", align_bytes=64)
             grouped_words = grouped[:].bitcast(F32)
             for pair in range(2):
-                xt = psum_xt.tile([P, 2, 2, P], F32, tag="xt")
+                xt = psum.tile([P, 2, 2, P], F32, tag="bank")
                 for h in range(2):
                     for u in range(2):
                         t = 2 * pair + h
@@ -124,13 +129,13 @@ def tile_gcn_pb_t_kernel(tc, x, ahat, gcn1_w, gcn1_b, out):
                 )
             x_grouped[g] = grouped
 
-        def first_matmul(g, c):
+        def first_matmul(g, c, on_vector):
             if c == 0:
                 grouped = rotating.tile([P, D_HID, PACK], BF16, tag="y_grouped", align_bytes=64)
                 y_grouped[g] = grouped
             codes, scales = x_codes[g]
             f_cols = slice(c * F_CHUNK, (c + 1) * F_CHUNK)
-            y_bank = psum_y.tile([P, PACK, F_CHUNK], F32, tag="y_bank")
+            y_bank = psum.tile([P, PACK, F_CHUNK], F32, tag="bank")
             for t in range(PACK):
                 n_cols = slice(t * P, (t + 1) * P)
                 nc.tensor.matmul_mx(
@@ -142,12 +147,15 @@ def tile_gcn_pb_t_kernel(tc, x, ahat, gcn1_w, gcn1_b, out):
                     start=True,
                     stop=True,
                 )
-            nc.scalar.copy(out=y_grouped[g][:, f_cols, :], in_=y_bank[:].rearrange("n t f -> n f t"))
+            if on_vector:
+                nc.vector.tensor_copy(out=y_grouped[g][:, f_cols, :], in_=y_bank[:].rearrange("n t f -> n f t"))
+            else:
+                nc.scalar.copy(out=y_grouped[g][:, f_cols, :], in_=y_bank[:].rearrange("n t f -> n f t"))
 
         def second_matmul(n):
             b = n // J_TILES
             j_cols = slice((n % J_TILES) * P, (n % J_TILES + 1) * P)
-            out_bank = psum_out.tile([P, D_HID], F32, tag="out_bank")
+            out_bank = psum.tile([P, D_HID], F32, tag="bank")
             for g in range(PASSES):
                 nc.tensor.matmul_mx(
                     out=out_bank[:],
@@ -169,11 +177,11 @@ def tile_gcn_pb_t_kernel(tc, x, ahat, gcn1_w, gcn1_b, out):
                 scales = adjacency.tile([P, NODES], U8, tag="a_scales", align_bytes=64)
                 a_grouped[g] = grouped
                 a_codes[g] = (codes, scales)
-            j_cols = slice(j_half * (NODES // 2), (j_half + 1) * (NODES // 2))
+            j_cols = slice(j_half * J_HALF, (j_half + 1) * J_HALF)
             regroup(a_grouped[g][:, j_cols, :], a_raw[g][:, :, j_cols])
 
         def quantise_adjacency(g, j_half):
-            j_cols = slice(j_half * (NODES // 2), (j_half + 1) * (NODES // 2))
+            j_cols = slice(j_half * J_HALF, (j_half + 1) * J_HALF)
             nc.vector.quantize_mx(
                 out=a_codes[g][0][:, j_cols].bitcast(FP8X4),
                 scales=a_codes[g][1][:, j_cols],
@@ -187,41 +195,53 @@ def tile_gcn_pb_t_kernel(tc, x, ahat, gcn1_w, gcn1_b, out):
                 nc.scalar.activation(out=result[n][:], in_=result[n][:], func=mybir.ActivationFunctionType.Relu)
             nc.sync.dma_start(out=out_rows[n * P : (n + 1) * P, :], in_=result[n][:])
 
-        transpose_x(0)
         w_grouped = consts.tile([P, D_HID, PACK], BF16, tag="w_grouped", align_bytes=64)
-        regroup(w_grouped[:], w_raw[:])
-        x_codes[0] = quantise(x_grouped[0][:], GROUP, rotating, "x")
-        w_codes, w_scales = quantise(w_grouped[:].rearrange("p c t -> p (c t)"), D_HID, consts, "w")
-        transpose_x(1)
-        bias_bank = psum_out.tile([P, D_HID], F32, tag="out_bank")
+        w_codes = consts.tile([P, D_HID], U32, tag="w_codes", align_bytes=64)
+        w_scales = consts.tile([P, D_HID], U8, tag="w_scales", align_bytes=64)
+
+        def w_half(i):
+            return slice(i * D_HID // 2, (i + 1) * D_HID // 2)
+
+        transpose_x(0)
+        for i in range(2):
+            regroup(w_grouped[:, w_half(i), :], w_raw[:, :, w_half(i)])
+        bias_bank = psum.tile([P, D_HID], F32, tag="bank")
         nc.tensor.matmul(out=bias_bank[:], lhsT=ones[:], rhs=bias_row[:], start=True, stop=True)
         bias_all = consts.tile([P, D_HID], F32, tag="bias_all")
         nc.scalar.copy(out=bias_all[:], in_=bias_bank[:])
+        x_codes[0] = quantise(x_grouped[0][:], GROUP, rotating, "x")
+        for i in range(2):
+            nc.vector.quantize_mx(
+                out=w_codes[:, w_half(i)].bitcast(FP8X4),
+                scales=w_scales[:, w_half(i)],
+                in_=w_grouped[:, w_half(i), :].rearrange("p c t -> p (c t)"),
+            )
+        transpose_x(1)
 
-        fresh_pieces = []
+        fresh_half = None
         for r in range(N_GROUPS + LAG):
             first_active = r < N_GROUPS
-            if 1 <= r <= N_GROUPS:
-                y_codes[r - 1] = quantise(y_grouped[r - 1][:].rearrange("p f t -> p (f t)"), D_HID, resident, "y")
             if r + 1 < N_GROUPS:
                 x_codes[r + 1] = quantise(x_grouped[r + 1][:], GROUP, rotating, "x")
-            for piece in fresh_pieces:
-                quantise_adjacency(*piece)
+            if 1 <= r <= N_GROUPS:
+                y_codes[r - 1] = quantise(y_grouped[r - 1][:].rearrange("p f t -> p (f t)"), D_HID, resident, "y")
+            if fresh_half is not None:
+                for g in range(PASSES):
+                    quantise_adjacency(g, fresh_half)
+            if r + AHEAD < N_GROUPS:
+                transpose_x(r + AHEAD)
             banks = [BANKS_PER_ROUND * (r - LAG) + i for i in range(BANKS_PER_ROUND)] if r >= LAG else []
             for half in range(2):
                 if first_active:
-                    first_matmul(r, 2 * half)
-                    first_matmul(r, 2 * half + 1)
+                    for c in (2 * half, 2 * half + 1):
+                        first_matmul(r, c, on_vector=(r < LAG and r % 2 == 1 and c == F_CHUNKS - 1))
                 for n in banks[2 * half : 2 * half + 2]:
                     second_matmul(n)
-            for n in banks:
-                relu_and_store(n, on_vector=(r + 1 < N_GROUPS and n % 2 == 1))
-            if r + AHEAD < N_GROUPS:
-                transpose_x(r + AHEAD)
-            fresh_pieces = []
-            if r == 0:
-                fresh_pieces = [(0, 0), (0, 1)]
-            if r == 1 or r == 2:
-                fresh_pieces = [(1, r - 1)]
-            for piece in fresh_pieces:
-                regroup_adjacency(*piece)
+            fresh_half = None
+            if r < LAG and r % 2 == 0:
+                fresh_half = r // 2
+                for g in range(PASSES):
+                    regroup_adjacency(g, fresh_half)
+            vector_relus = max(0, N_GROUPS - 1 - r)
+            for i, n in enumerate(banks):
+                relu_and_store(n, on_vector=(i >= BANKS_PER_ROUND - vector_relus))

@@ -69,11 +69,10 @@ def tile_gcn_pb_t_kernel(tc, x, ahat, gcn1_w, gcn1_b, out):
         def load_adjacency(half):
             j_cols = slice(half * J_HALF, (half + 1) * J_HALF)
             for g in range(PASSES):
-                if half == 0:
-                    raw = adjacency.tile([P, PACK, NODES], BF16, tag="a_raw")
-                    a_raw[g] = raw
+                raw = adjacency.tile([P, PACK, J_HALF], BF16, tag="a_raw", bufs=PASSES * HALVES)
                 rows = ahat[g * K_PASS : (g + 1) * K_PASS, :].rearrange("(p t) j -> p t j", t=PACK)
-                nc.sync.dma_start(out=a_raw[g][:, :, j_cols], in_=rows[:, :, j_cols])
+                nc.sync.dma_start(out=raw[:], in_=rows[:, :, j_cols])
+                a_raw[g, half] = raw
 
         bias_row = consts.tile([P, D_HID], BF16, tag="bias_row")
         nc.vector.memset(bias_row[:], 0.0)
@@ -178,7 +177,7 @@ def tile_gcn_pb_t_kernel(tc, x, ahat, gcn1_w, gcn1_b, out):
                 a_grouped[g] = grouped
                 a_codes[g] = (codes, scales)
             j_cols = slice(j_half * J_HALF, (j_half + 1) * J_HALF)
-            regroup(a_grouped[g][:, j_cols, :], a_raw[g][:, :, j_cols])
+            regroup(a_grouped[g][:, j_cols, :], a_raw[g, j_half][:])
 
         def quantise_adjacency(g, j_half):
             j_cols = slice(j_half * J_HALF, (j_half + 1) * J_HALF)

@@ -74,13 +74,9 @@ def tile_gcn_pb_t_kernel(tc, x, ahat, gcn1_w, gcn1_b, out):
                 nc.sync.dma_start(out=raw[:], in_=rows[:, :, j_cols])
                 a_raw[g, half] = raw
 
-        bias_row = consts.tile([P, D_HID], BF16, tag="bias_row")
-        nc.vector.memset(bias_row[:], 0.0)
-
         load_x(0, pieces=2)
         w_raw = consts.tile([P, PACK, D_HID], BF16, tag="w_raw")
         nc.sync.dma_start(out=w_raw[:], in_=gcn1_w.rearrange("(q t) c -> q t c", t=PACK))
-        nc.sync.dma_start(out=bias_row[0:1, :], in_=gcn1_b.unsqueeze(0))
         load_x(1)
         load_x(2)
         load_adjacency(0)
@@ -88,11 +84,11 @@ def tile_gcn_pb_t_kernel(tc, x, ahat, gcn1_w, gcn1_b, out):
         load_adjacency(1)
         for g in range(4, N_GROUPS):
             load_x(g)
+        bias_all = consts.tile([P, D_HID], BF16, tag="bias_all")
+        nc.sync.dma_start(out=bias_all[:], in_=gcn1_b.partition_broadcast(P))
 
         identity = consts.tile([P, P], F32, tag="identity")
         make_identity(nc, identity[:])
-        ones = consts.tile([P, P], BF16, tag="ones")
-        nc.vector.memset(ones[:], 1.0)
         warm = consts.tile([P, 1], F32, tag="warm")
         nc.vector.memset(warm[:], 0.0)
         nc.scalar.activation(out=warm[:], in_=warm[:], func=mybir.ActivationFunctionType.Relu)
@@ -204,10 +200,6 @@ def tile_gcn_pb_t_kernel(tc, x, ahat, gcn1_w, gcn1_b, out):
         transpose_x(0)
         for i in range(2):
             regroup(w_grouped[:, w_half(i), :], w_raw[:, :, w_half(i)])
-        bias_bank = psum.tile([P, D_HID], F32, tag="bank")
-        nc.tensor.matmul(out=bias_bank[:], lhsT=ones[:], rhs=bias_row[:], start=True, stop=True)
-        bias_all = consts.tile([P, D_HID], F32, tag="bias_all")
-        nc.scalar.copy(out=bias_all[:], in_=bias_bank[:])
         x_codes[0] = quantise(x_grouped[0][:], GROUP, rotating, "x")
         for i in range(2):
             nc.vector.quantize_mx(

@@ -43,7 +43,7 @@ def tile_gcn_pb_t_kernel(tc, x, ahat, gcn1_w, gcn1_b, out):
         adjacency = stack.enter_context(tc.tile_pool(name="adjacency", bufs=PASSES))
         resident = stack.enter_context(tc.tile_pool(name="resident", bufs=N_GROUPS))
         rotating = stack.enter_context(tc.tile_pool(name="rotating", bufs=3))
-        results = stack.enter_context(tc.tile_pool(name="results", bufs=3 * BANKS_PER_ROUND))
+        results = stack.enter_context(tc.tile_pool(name="results", bufs=N_BANKS))
         psum = stack.enter_context(tc.psum_pool(name="psum", bufs=8))
         stack.enter_context(tc.manual_schedule())
 
@@ -200,7 +200,7 @@ def tile_gcn_pb_t_kernel(tc, x, ahat, gcn1_w, gcn1_b, out):
         transpose_x(0)
         for i in range(2):
             regroup(w_grouped[:, w_half(i), :], w_raw[:, :, w_half(i)])
-        x_codes[0] = quantise(x_grouped[0][:], GROUP, rotating, "x")
+        x_codes[0] = quantise(x_grouped[0][:], GROUP, resident, "x")
         for i in range(2):
             nc.vector.quantize_mx(
                 out=w_codes[:, w_half(i)].bitcast(FP8X4),
@@ -213,7 +213,7 @@ def tile_gcn_pb_t_kernel(tc, x, ahat, gcn1_w, gcn1_b, out):
         for r in range(N_GROUPS + LAG):
             first_active = r < N_GROUPS
             if r + 1 < N_GROUPS:
-                x_codes[r + 1] = quantise(x_grouped[r + 1][:], GROUP, rotating, "x")
+                x_codes[r + 1] = quantise(x_grouped[r + 1][:], GROUP, resident, "x")
             if 1 <= r <= N_GROUPS:
                 y_codes[r - 1] = quantise(y_grouped[r - 1][:].rearrange("p f t -> p (f t)"), D_HID, resident, "y")
             if fresh_half is not None:

@@ -25,7 +25,7 @@ F_CHUNK = 128
 F_CHUNKS = D_HID // F_CHUNK
 J_TILES = NODES // P
 N_BANKS = GRAPHS * J_TILES
-BANKS_PER_ROUND = N_BANKS // N_GROUPS
+BANKS_IN_ROUND = (0, 0, 0, 0, 5, 5, 5, 5, 4, 4, 4)
 AHEAD = 2
 LAG = 4
 HALVES = 2
@@ -77,12 +77,13 @@ def tile_gcn_pb_t_kernel(tc, x, ahat, gcn1_w, gcn1_b, out):
         load_x(0, pieces=2)
         w_raw = consts.tile([P, PACK, D_HID], BF16, tag="w_raw")
         nc.sync.dma_start(out=w_raw[:], in_=gcn1_w.rearrange("(q t) c -> q t c", t=PACK))
-        load_x(1)
+        load_x(1, pieces=2)
         load_x(2)
         load_adjacency(0)
         load_x(3)
+        load_x(4)
         load_adjacency(1)
-        for g in range(4, N_GROUPS):
+        for g in range(5, N_GROUPS):
             load_x(g)
         bias_all = consts.tile([P, D_HID], BF16, tag="bias_all")
         nc.sync.dma_start(out=bias_all[:], in_=gcn1_b.partition_broadcast(P))
@@ -210,7 +211,8 @@ def tile_gcn_pb_t_kernel(tc, x, ahat, gcn1_w, gcn1_b, out):
         transpose_x(1)
 
         fresh_half = None
-        for r in range(N_GROUPS + LAG):
+        n_next = 0
+        for r, n_banks in enumerate(BANKS_IN_ROUND):
             first_active = r < N_GROUPS
             if r + 1 < N_GROUPS:
                 x_codes[r + 1] = quantise(x_grouped[r + 1][:], GROUP, resident, "x")
@@ -221,18 +223,19 @@ def tile_gcn_pb_t_kernel(tc, x, ahat, gcn1_w, gcn1_b, out):
                     quantise_adjacency(g, fresh_half)
             if r + AHEAD < N_GROUPS:
                 transpose_x(r + AHEAD)
-            banks = [BANKS_PER_ROUND * (r - LAG) + i for i in range(BANKS_PER_ROUND)] if r >= LAG else []
+            banks = list(range(n_next, n_next + n_banks))
+            n_next += n_banks
             for half in range(2):
                 if first_active:
                     for c in (2 * half, 2 * half + 1):
                         first_matmul(r, c, on_vector=(r < LAG and r % 2 == 1 and c == F_CHUNKS - 1))
-                for n in banks[2 * half : 2 * half + 2]:
+                for n in banks[: n_banks // 2] if half == 0 else banks[n_banks // 2 :]:
                     second_matmul(n)
             fresh_half = None
             if r < LAG and r % 2 == 0:
                 fresh_half = r // 2
                 for g in range(PASSES):
                     regroup_adjacency(g, fresh_half)
-            vector_relus = max(0, N_GROUPS - 1 - r)
+            vector_relus = 2 if r < N_GROUPS - 1 else 0
             for i, n in enumerate(banks):
-                relu_and_store(n, on_vector=(i >= BANKS_PER_ROUND - vector_relus))
+                relu_and_store(n, on_vector=(i >= n_banks - vector_relus))

from contextlib import ExitStack

import concourse.mybir as mybir
from concourse.masks import make_identity

F32 = mybir.dt.float32
BF16 = mybir.dt.bfloat16
U32 = mybir.dt.uint32
U8 = mybir.dt.uint8
FP8X4 = mybir.dt.float8_e4m3fn_x4

P = 128
PACK = 4
K_PASS = P * PACK

GRAPHS = 4
NODES = 1024
D_IN = 512
D_HID = 512

GROUP = K_PASS
N_GROUPS = GRAPHS * NODES // GROUP
PASSES = NODES // K_PASS
F_CHUNK = 128
F_CHUNKS = D_HID // F_CHUNK
J_TILES = NODES // P
N_BANKS = GRAPHS * J_TILES
BANKS_IN_ROUND = (0, 0, 0, 0, 5, 5, 5, 5, 4, 4, 4)
AHEAD = 2
LAG = 4
HALVES = 2
J_HALF = NODES // HALVES

FLOPS = 2 * GRAPHS * NODES * D_IN * D_HID + 2 * GRAPHS * NODES * NODES * D_HID


def tile_gcn_pb_t_kernel(tc, x, ahat, gcn1_w, gcn1_b, out):
    nc = tc.nc
    out_rows = out.flatten_outer_dims()

    with ExitStack() as stack:
        consts = stack.enter_context(tc.tile_pool(name="consts", bufs=1))
        adjacency = stack.enter_context(tc.tile_pool(name="adjacency", bufs=PASSES))
        resident = stack.enter_context(tc.tile_pool(name="resident", bufs=N_GROUPS))
        rotating = stack.enter_context(tc.tile_pool(name="rotating", bufs=3))
        results = stack.enter_context(tc.tile_pool(name="results", bufs=N_BANKS))
        psum = stack.enter_context(tc.psum_pool(name="psum", bufs=8))
        stack.enter_context(tc.manual_schedule())

        x_raw = {}
        x_grouped = {}
        x_codes = {}
        y_grouped = {}
        y_codes = {}
        a_raw = {}
        a_grouped = {}
        a_codes = {}
        result = {}

        def load_x(g, pieces=1):
            raw = resident.tile([P, PACK * D_IN], BF16, tag="x_raw")
            group = x[g * GROUP : (g + 1) * GROUP, :].rearrange("(p t) k -> p (t k)", t=PACK)
            width = PACK * D_IN // pieces
            for i in range(pieces):
                cols = slice(i * width, (i + 1) * width)
                nc.sync.dma_start(out=raw[:, cols], in_=group[:, cols])
            x_raw[g] = raw

        def load_adjacency(half):
            j_cols = slice(half * J_HALF, (half + 1) * J_HALF)
            for g in range(PASSES):
                raw = adjacency.tile([P, PACK, J_HALF], BF16, tag="a_raw", bufs=PASSES * HALVES)
                rows = ahat[g * K_PASS : (g + 1) * K_PASS, :].rearrange("(p t) j -> p t j", t=PACK)
                nc.sync.dma_start(out=raw[:], in_=rows[:, :, j_cols])
                a_raw[g, half] = raw

        load_x(0, pieces=2)
        w_raw = consts.tile([P, PACK, D_HID], BF16, tag="w_raw")
        nc.sync.dma_start(out=w_raw[:], in_=gcn1_w.rearrange("(q t) c -> q t c", t=PACK))
        load_x(1, pieces=2)
        load_x(2)
        load_adjacency(0)
        load_x(3)
        load_x(4)
        load_adjacency(1)
        for g in range(5, N_GROUPS):
            load_x(g)
        bias_all = consts.tile([P, D_HID], BF16, tag="bias_all")
        nc.sync.dma_start(out=bias_all[:], in_=gcn1_b.partition_broadcast(P))

        identity = consts.tile([P, P], F32, tag="identity")
        make_identity(nc, identity[:])
        warm = consts.tile([P, 1], F32, tag="warm")
        nc.vector.memset(warm[:], 0.0)
        nc.scalar.activation(out=warm[:], in_=warm[:], func=mybir.ActivationFunctionType.Relu)

        def regroup(dst, src):
            nc.vector.tensor_copy(
                out=dst.rearrange("p (c i) t -> p c t i", i=4), in_=src.rearrange("p t (c i) -> p c t i", i=4)
            )

        def quantise(grouped, width, pool, tag):
            codes = pool.tile([P, width], U32, tag=tag + "_codes", align_bytes=64)
            scales = pool.tile([P, width], U8, tag=tag + "_scales", align_bytes=64)
            nc.vector.quantize_mx(out=codes[:].bitcast(FP8X4), scales=scales[:], in_=grouped)
            return codes, scales

        def transpose_x(g):
            words = x_raw[g][:].bitcast(F32)
            grouped = rotating.tile([P, PACK * GROUP], BF16, tag="x_grouped", align_bytes=64)
            grouped_words = grouped[:].bitcast(F32)
            for pair in range(2):
                xt = psum.tile([P, 2, 2, P], F32, tag="bank")
                for h in range(2):
                    for u in range(2):
                        t = 2 * pair + h
                        nc.tensor.transpose(
                            xt[:, h, u, :], words[:, t * 256 + u : (t + 1) * 256 : 2], identity[:]
                        )
                nc.scalar.copy(
                    out=grouped_words[:, pair * 512 : (pair + 1) * 512].rearrange(
                        "q (h n u) -> q h n u", h=2, n=P, u=2
                    ),
                    in_=xt[:].rearrange("q h u n -> q h n u"),
                )
            x_grouped[g] = grouped

        def first_matmul(g, c, on_vector):
            if c == 0:
                grouped = rotating.tile([P, D_HID, PACK], BF16, tag="y_grouped", align_bytes=64)
                y_grouped[g] = grouped
            codes, scales = x_codes[g]
            f_cols = slice(c * F_CHUNK, (c + 1) * F_CHUNK)
            y_bank = psum.tile([P, PACK, F_CHUNK], F32, tag="bank")
            for t in range(PACK):
                n_cols = slice(t * P, (t + 1) * P)
                nc.tensor.matmul_mx(
                    out=y_bank[:, t, :],
                    lhsT=codes[:, n_cols].bitcast(FP8X4),
                    lhsT_scale=scales[:, n_cols],
                    rhs=w_codes[:, f_cols].bitcast(FP8X4),
                    rhs_scale=w_scales[:, f_cols],
                    start=True,
                    stop=True,
                )
            if on_vector:
                nc.vector.tensor_copy(out=y_grouped[g][:, f_cols, :], in_=y_bank[:].rearrange("n t f -> n f t"))
            else:
                nc.scalar.copy(out=y_grouped[g][:, f_cols, :], in_=y_bank[:].rearrange("n t f -> n f t"))

        def second_matmul(n):
            b = n // J_TILES
            j_cols = slice((n % J_TILES) * P, (n % J_TILES + 1) * P)
            out_bank = psum.tile([P, D_HID], F32, tag="bank")
            for g in range(PASSES):
                nc.tensor.matmul_mx(
                    out=out_bank[:],
                    lhsT=a_codes[g][0][:, j_cols].bitcast(FP8X4),
                    lhsT_scale=a_codes[g][1][:, j_cols],
                    rhs=y_codes[PASSES * b + g][0][:].bitcast(FP8X4),
                    rhs_scale=y_codes[PASSES * b + g][1][:],
                    start=(g == 0),
                    stop=(g == PASSES - 1),
                )
            biased = results.tile([P, D_HID], F32, tag="result")
            nc.vector.tensor_tensor(out=biased[:], in0=out_bank[:], in1=bias_all[:], op=mybir.AluOpType.add)
            result[n] = biased

        def regroup_adjacency(g, j_half):
            if j_half == 0:
                grouped = adjacency.tile([P, NODES, PACK], BF16, tag="a_grouped", align_bytes=64)
                codes = adjacency.tile([P, NODES], U32, tag="a_codes", align_bytes=64)
                scales = adjacency.tile([P, NODES], U8, tag="a_scales", align_bytes=64)
                a_grouped[g] = grouped
                a_codes[g] = (codes, scales)
            j_cols = slice(j_half * J_HALF, (j_half + 1) * J_HALF)
            regroup(a_grouped[g][:, j_cols, :], a_raw[g, j_half][:])

        def quantise_adjacency(g, j_half):
            j_cols = slice(j_half * J_HALF, (j_half + 1) * J_HALF)
            nc.vector.quantize_mx(
                out=a_codes[g][0][:, j_cols].bitcast(FP8X4),
                scales=a_codes[g][1][:, j_cols],
                in_=a_grouped[g][:, j_cols, :].rearrange("p j t -> p (j t)"),
            )

        def relu_and_store(n, on_vector):
            if on_vector:
                nc.vector.tensor_scalar_max(out=result[n][:], in0=result[n][:], scalar1=0.0)
            else:
                nc.scalar.activation(out=result[n][:], in_=result[n][:], func=mybir.ActivationFunctionType.Relu)
            nc.sync.dma_start(out=out_rows[n * P : (n + 1) * P, :], in_=result[n][:])

        w_grouped = consts.tile([P, D_HID, PACK], BF16, tag="w_grouped", align_bytes=64)
        w_codes = consts.tile([P, D_HID], U32, tag="w_codes", align_bytes=64)
        w_scales = consts.tile([P, D_HID], U8, tag="w_scales", align_bytes=64)

        def w_half(i):
            return slice(i * D_HID // 2, (i + 1) * D_HID // 2)

        transpose_x(0)
        for i in range(2):
            regroup(w_grouped[:, w_half(i), :], w_raw[:, :, w_half(i)])
        x_codes[0] = quantise(x_grouped[0][:], GROUP, resident, "x")
        for i in range(2):
            nc.vector.quantize_mx(
                out=w_codes[:, w_half(i)].bitcast(FP8X4),
                scales=w_scales[:, w_half(i)],
                in_=w_grouped[:, w_half(i), :].rearrange("p c t -> p (c t)"),
            )
        transpose_x(1)

        fresh_half = None
        n_next = 0
        for r, n_banks in enumerate(BANKS_IN_ROUND):
            first_active = r < N_GROUPS
            if r + 1 < N_GROUPS:
                x_codes[r + 1] = quantise(x_grouped[r + 1][:], GROUP, resident, "x")
            if 1 <= r <= N_GROUPS:
                y_codes[r - 1] = quantise(y_grouped[r - 1][:].rearrange("p f t -> p (f t)"), D_HID, resident, "y")
            if fresh_half is not None:
                for g in range(PASSES):
                    quantise_adjacency(g, fresh_half)
            if r + AHEAD < N_GROUPS:
                transpose_x(r + AHEAD)
            banks = list(range(n_next, n_next + n_banks))
            n_next += n_banks
            for half in range(2):
                if first_active:
                    for c in (2 * half, 2 * half + 1):
                        first_matmul(r, c, on_vector=(r < LAG and r % 2 == 1 and c == F_CHUNKS - 1))
                for n in banks[: n_banks // 2] if half == 0 else banks[n_banks // 2 :]:
                    second_matmul(n)
            fresh_half = None
            if r < LAG and r % 2 == 0:
                fresh_half = r // 2
                for g in range(PASSES):
                    regroup_adjacency(g, fresh_half)
            vector_relus = 2 if r < N_GROUPS - 1 else 0
            for i, n in enumerate(banks):
                relu_and_store(n, on_vector=(i >= n_banks - vector_relus))
